import numpy as np
import ml_dtypes


def mxq(x, axis, fmt="e4m3"):
    dtype, down = {"e4m3": (ml_dtypes.float8_e4m3fn, 7), "e5m2": (ml_dtypes.float8_e5m2, 14)}[fmt]
    v = np.moveaxis(np.asarray(x, np.float32).astype(ml_dtypes.bfloat16).astype(np.float64), axis, -1)
    blocks = v.reshape(v.shape[:-1] + (-1, 32))
    amax = np.abs(blocks).max(-1, keepdims=True)
    byte = np.maximum(np.where(amax > 0, np.frexp(amax)[1] - 1 + 127, 0) - down, 1)
    scale = np.exp2(byte - 127.0)
    codes = (blocks / scale).astype(np.float32).astype(dtype).astype(np.float64)
    return np.moveaxis((codes * scale).reshape(v.shape), -1, axis)


WIDE = False


def mx_kscale(k):
    if not WIDE:
        return np.ones(k)
    levels = np.array([10, -10, 5, -5, 0])
    a = np.random.permutation(np.resize(levels, k // 512 * 4)).reshape(k // 512, 4)
    idx = np.arange(k)
    return np.exp2(a[idx // 512, idx % 128 // 32])


BF16 = ml_dtypes.bfloat16


def bf(x):
    return np.asarray(x, np.float32).astype(BF16)


def f64(x):
    return np.asarray(x).astype(np.float64)


E2M1 = np.array([0.0, 0.5, 1.0, 1.5, 2.0, 3.0, 4.0, 6.0, -0.0, -0.5, -1.0, -1.5, -2.0, -3.0, -4.0, -6.0])


def pack_weight(w, fmt):
    k, n = w.shape
    w = f64(bf(w)).reshape(k // 32, 32, n)
    amax = np.abs(w).max(1)
    if fmt == "e4m3":
        byte = np.frexp(amax)[1] - 1 + 127 - 7
    else:
        mant, ex = np.frexp(amax / 6.0)
        byte = np.where(mant > 0.5, ex, ex - 1) + 127
    byte = np.clip(np.where(amax > 0, byte, 1), 1, 254)
    scaled = (w * np.exp2(127.0 - byte)[:, None, :]).reshape(k, n).astype(np.float32)
    by_word = np.ascontiguousarray(scaled.reshape(k // 512, 128, 4, n).transpose(0, 1, 3, 2))
    if fmt == "e4m3":
        words = by_word.astype(ml_dtypes.float8_e4m3fn).view(np.uint8)
    else:
        c = by_word.astype(ml_dtypes.float4_e2m1fn).view(np.uint8) & 0xF
        words = c[..., 0::2] | (c[..., 1::2] << 4)
    return np.ascontiguousarray(words), np.ascontiguousarray(byte.astype(np.uint8).reshape(k // 512, 16, n))


def unpack_weight(words, scales, fmt):
    g, p, n, _ = words.shape
    if fmt == "e4m3":
        vals = np.ascontiguousarray(words).view(ml_dtypes.float8_e4m3fn).astype(np.float64)
    else:
        nib = np.empty((g, p, n, 4), np.uint8)
        nib[..., 0::2] = words & 0xF
        nib[..., 1::2] = words >> 4
        vals = E2M1[nib]
    vals = vals * np.repeat(np.exp2(scales.astype(np.float64) - 127.0), 8, axis=1)[..., None]
    return vals.transpose(0, 1, 3, 2).reshape(g * 512, n)

def pack4(w):
    words, scales = pack_weight(w, "e2m1")
    return words.reshape(words.shape[0], 128, -1), scales


def unpack4(words, scales):
    return unpack_weight(words.reshape(words.shape[0], 128, -1, 2), scales, "e2m1")


B, T, D, H, NUM_LAYERS = 4, 2048, 512, 512, 3
EPS = 1e-8


def setup_inputs():
    s = mx_kscale(D)
    inv = bf(np.random.standard_normal((B, T, D)) * 0.5 * s)
    Wk = np.random.standard_normal((D, D)) * 2.0 / np.sqrt(D) / s[None, :]
    words, scales = pack4(np.ascontiguousarray(Wk.T))
    bk = bf(2.5 / np.sqrt(D) + 0.7 * np.random.standard_normal(D))
    return {"inv": inv,
            "Wk_words": words,
            "Wk_scales": scales,
            "bk": bk}


def reference(inv, Wk_words, Wk_scales, bk):
    flat = f64(inv).reshape(-1, D)
    out = (mxq(flat, 1, "e4m3") @ unpack4(Wk_words, Wk_scales)) + f64(bk)
    sqrtD = np.sqrt(D)
    S = out.sum(-1, keepdims=True)
    norms = np.sqrt((out * out).sum(-1, keepdims=True))
    c = out * S / (np.maximum(np.abs(out) * sqrtD, EPS) * np.maximum(norms, EPS))
    diff = np.abs(c[1:] - c[:-1]).sum(0)
    return np.broadcast_to(diff, (D, D)).copy()

@@ -1,0 +1,206 @@
+import math
+
+import concourse.mybir as mybir
+from concourse.masks import make_identity
+
+F32 = mybir.dt.float32
+BF16 = mybir.dt.bfloat16
+I32 = mybir.dt.int32
+U32 = mybir.dt.uint32
+U8 = mybir.dt.uint8
+FP8X4 = mybir.dt.float8_e4m3fn_x4
+FP4X4 = mybir.dt.float4_e2m1fn_x4
+ALU = mybir.AluOpType
+ACT = mybir.ActivationFunctionType
+
+P = 128
+PACK = 4
+D = 512
+TOKENS = 8192
+TILES = TOKENS // P
+GROUP = 4
+GROUPS = TILES // GROUP
+SLICES = D // P
+WORDS = D // 2
+EPS = 1e-8
+CLIP = EPS / math.sqrt(D)
+
+FLOPS = 2 * TOKENS * D * D
+
+
+def tile_dispatcher_pa_kernel(tc, inv, Wk_words, Wk_scales, bk, out):
+    nc = tc.nc
+    tokens = inv.flatten_outer_dims().rearrange("(p j) k -> p j k", j=TILES)
+
+    with tc.tile_pool(name="const", bufs=1) as const, tc.tile_pool(
+        name="keep", bufs=1
+    ) as keep, tc.tile_pool(name="xin", bufs=1) as xin, tc.tile_pool(
+        name="stage", bufs=2
+    ) as stage, tc.tile_pool(name="stats", bufs=3) as stats, tc.psum_pool(
+        name="psum_x", bufs=2
+    ) as psum_x, tc.psum_pool(name="psum_mx", bufs=2) as psum_mx, tc.psum_pool(
+        name="psum_e", bufs=4
+    ) as psum_e:
+        ident2 = const.tile([P, 2 * P], F32)
+        make_identity(nc, ident2[:, 0:P])
+        make_identity(nc, ident2[:, P : 2 * P])
+        ident = ident2[:, 0:P]
+        ident_next = ident2[:, 1 : P + 1]
+
+        w_words = const.tile([P, 2 * D], U8, align_bytes=64)
+        w_plane = const.tile([P, D], U8, align_bytes=64)
+        bias = const.tile([P, D], BF16)
+        nc.vector.memset(w_plane[:].bitcast(I32), 0)
+
+        x_tiles = []
+        for g in range(GROUPS):
+            x_sb = xin.tile([P, GROUP, D], BF16, name="x%d" % g)
+            nc.sync.dma_start(out=x_sb[:], in_=tokens[:, g * GROUP : (g + 1) * GROUP, :])
+            x_tiles.append(x_sb)
+            if g == 0:
+                nc.sync.dma_start(out=w_words[:].bitcast(I32), in_=Wk_words[0].bitcast(I32))
+                for q in range(4):
+                    nc.sync.dma_start(
+                        out=w_plane[32 * q : 32 * q + 4, :].bitcast(I32),
+                        in_=Wk_scales[0, 4 * q : 4 * q + 4, :].bitcast(I32),
+                    )
+                nc.sync.dma_start(out=bias[:], in_=bk.partition_broadcast(P))
+
+        rows = [keep.tile([P, GROUP, D], F32, name="rows%d" % g) for g in range(GROUPS)]
+        part = keep.tile([P, SLICES, GROUPS], F32)
+
+        def row_tile(j):
+            return rows[j // GROUP][:, j % GROUP, :]
+
+        def quantise(g):
+            x_words = x_tiles[g][:].bitcast(F32)
+            grouped = stage.tile([P, GROUP, P, PACK], BF16, align_bytes=64)
+            grouped_words = grouped[:].bitcast(F32)
+            for half in range(GROUP // 2):
+                xt = psum_x.tile([P, 2, 2, P], F32)
+                for a in range(2):
+                    for u in range(2):
+                        nc.tensor.transpose(
+                            xt[:, a, u, :], x_words[:, 2 * half + a, u:WORDS:2], ident
+                        )
+                nc.scalar.copy(
+                    out=grouped_words[:, 2 * half : 2 * half + 2, :, :],
+                    in_=xt[:].rearrange("p a u r -> p a r u"),
+                )
+            codes = stage.tile([P, GROUP * P], U32, align_bytes=64)
+            plane = stage.tile([P, GROUP * P], U8, align_bytes=64)
+            nc.vector.quantize_mx(
+                out=codes[:].bitcast(FP8X4),
+                scales=plane[:],
+                in_=grouped[:].rearrange("p a r t -> p (a r t)"),
+            )
+            return codes, plane
+
+        def multiply(g, codes, plane):
+            row_sum = stats.tile([P, GROUP], F32)
+            row_sq = stats.tile([P, GROUP], F32)
+            for a in range(GROUP):
+                acc = psum_mx.tile([P, D], F32)
+                nc.tensor.matmul_mx(
+                    out=acc[:],
+                    lhsT=codes[:, a * P : (a + 1) * P].bitcast(FP8X4),
+                    lhsT_scale=plane[:, a * P : (a + 1) * P],
+                    rhs=w_words[:].bitcast(FP4X4),
+                    rhs_scale=w_plane[:],
+                    start=True,
+                    stop=True,
+                )
+                nc.vector.scalar_tensor_tensor(
+                    out=rows[g][:, a, :],
+                    in0=acc[:],
+                    scalar=1.0,
+                    in1=bias[:],
+                    op0=ALU.mult,
+                    op1=ALU.add,
+                    accum_out=row_sum[:, a : a + 1],
+                )
+                squares = stage.tile([P, D], F32, tag="unread")
+                nc.scalar.activation(
+                    out=squares[:],
+                    in_=rows[g][:, a, :],
+                    func=ACT.Square,
+                    accum_out=row_sq[:, a : a + 1],
+                )
+            return row_sum, row_sq
+
+        def scale_rows(g, row_sum, row_sq):
+            floored = stats.tile([P, GROUP], F32)
+            nc.vector.tensor_scalar_max(out=floored[:], in0=row_sq[:], scalar1=EPS * EPS)
+            norm = stats.tile([P, GROUP], F32)
+            nc.scalar.activation(out=norm[:], in_=floored[:], func=ACT.Sqrt)
+            nc.vector.tensor_scalar(
+                out=rows[g][:],
+                in0=rows[g][:],
+                scalar1=CLIP,
+                scalar2=-CLIP,
+                op0=ALU.min,
+                op1=ALU.max,
+            )
+            inv_norm = stats.tile([P, GROUP], F32)
+            nc.vector.reciprocal(out=inv_norm[:], in_=norm[:])
+            weight = stats.tile([P, GROUP], F32)
+            nc.vector.tensor_mul(out=weight[:], in0=row_sum[:], in1=inv_norm[:])
+            for a in range(GROUP):
+                sign = 1.0 if (g * GROUP + a) % 2 == 0 else -1.0
+                nc.vector.tensor_scalar(
+                    out=rows[g][:, a, :],
+                    in0=rows[g][:, a, :],
+                    scalar1=weight[:, a : a + 1],
+                    scalar2=sign / EPS,
+                    op0=ALU.mult,
+                    op1=ALU.mult,
+                )
+
+        def sum_differences(b):
+            for s in range(SLICES):
+                cols = slice(s * P, (s + 1) * P)
+                et = psum_e.tile([P, GROUP, P], F32)
+                for i in range(GROUP):
+                    j = b * GROUP + i
+                    nc.tensor.matmul(
+                        out=et[:, i, :],
+                        lhsT=row_tile(j)[:, cols],
+                        rhs=ident,
+                        is_transpose=True,
+                        start=True,
+                        stop=False,
+                    )
+                    nc.tensor.matmul(
+                        out=et[:, i, :],
+                        lhsT=row_tile((j + 1) % TILES)[:, cols],
+                        rhs=ident if j + 1 < TILES else ident_next,
+                        is_transpose=True,
+                        start=False,
+                        stop=True,
+                    )
+                used = GROUP * P if b + 1 < GROUPS else GROUP * P - 1
+                sizes = stage.tile([P, GROUP * P], F32, tag="unread")
+                nc.scalar.activation(
+                    out=sizes[:, 0:used],
+                    in_=et[:].rearrange("p i r -> p (i r)")[:, 0:used],
+                    func=ACT.Abs,
+                    accum_out=part[:, s, b : b + 1],
+                )
+
+        for g in range(GROUPS):
+            codes, plane = quantise(g)
+            row_sum, row_sq = multiply(g, codes, plane)
+            scale_rows(g, row_sum, row_sq)
+            if g >= 1:
+                sum_differences(g - 1)
+        sum_differences(GROUPS - 1)
+
+        total = keep.tile([P, SLICES], F32)
+        nc.vector.tensor_reduce(out=total[:], in_=part[:], axis=mybir.AxisListType.X, op=ALU.add)
+        spread = psum_e.tile([P, SLICES, P], F32, tag="et")
+        for s in range(SLICES):
+            nc.tensor.transpose(spread[:, s, :], total[:, s : s + 1].to_broadcast([P, P]), ident)
+        result = keep.tile([P, D], F32)
+        nc.vector.tensor_copy(out=result[:], in_=spread[:].rearrange("p s r -> p (s r)"))
+        for r in range(D // P):
+            nc.sync.dma_start(out=out[r * P : (r + 1) * P, :], in_=result[:])

@@ -20,6 +20,10 @@ TOKENS = 8192
 TILES = TOKENS // P
 GROUP = 4
 GROUPS = TILES // GROUP
+DUO = 2
+DUOS = TILES // DUO
+AHEAD = 2
+DIFF_LAG = 5
 SLICES = D // P
 WORDS = D // 2
 EPS = 1e-8
@@ -34,13 +38,11 @@ def tile_dispatcher_pa_kernel(tc, inv, Wk_words, Wk_scales, bk, out):
 
     with tc.tile_pool(name="const", bufs=1) as const, tc.tile_pool(
         name="keep", bufs=1
-    ) as keep, tc.tile_pool(name="xin", bufs=1) as xin, tc.tile_pool(
-        name="stage", bufs=2
-    ) as stage, tc.tile_pool(name="stats", bufs=3) as stats, tc.psum_pool(
-        name="psum_x", bufs=2
-    ) as psum_x, tc.psum_pool(name="psum_mx", bufs=2) as psum_mx, tc.psum_pool(
-        name="psum_e", bufs=4
-    ) as psum_e:
+    ) as keep, tc.tile_pool(name="stage", bufs=4) as stage, tc.tile_pool(
+        name="stats", bufs=3
+    ) as stats, tc.psum_pool(name="psum_x", bufs=2) as psum_x, tc.psum_pool(
+        name="psum_mx", bufs=2
+    ) as psum_mx, tc.psum_pool(name="psum_e", bufs=4) as psum_e, tc.manual_schedule():
         ident2 = const.tile([P, 2 * P], F32)
         make_identity(nc, ident2[:, 0:P])
         make_identity(nc, ident2[:, P : 2 * P])
@@ -52,9 +54,13 @@ def tile_dispatcher_pa_kernel(tc, inv, Wk_words, Wk_scales, bk, out):
         bias = const.tile([P, D], BF16)
         nc.vector.memset(w_plane[:].bitcast(I32), 0)
 
+        one = const.tile([P, 1], F32)
+        nc.vector.memset(one[:], 1.0)
+        nc.scalar.activation(out=one[:], in_=one[:], func=ACT.Sqrt)
+
         x_tiles = []
         for g in range(GROUPS):
-            x_sb = xin.tile([P, GROUP, D], BF16, name="x%d" % g)
+            x_sb = keep.tile([P, GROUP, D], BF16, name="x%d" % g)
             nc.sync.dma_start(out=x_sb[:], in_=tokens[:, g * GROUP : (g + 1) * GROUP, :])
             x_tiles.append(x_sb)
             if g == 0:
@@ -68,38 +74,43 @@ def tile_dispatcher_pa_kernel(tc, inv, Wk_words, Wk_scales, bk, out):
 
         rows = [keep.tile([P, GROUP, D], F32, name="rows%d" % g) for g in range(GROUPS)]
         part = keep.tile([P, SLICES, GROUPS], F32)
+        quantised = {}
+        row_sum = {}
+        row_sq = {}
+        norm = {}
 
         def row_tile(j):
             return rows[j // GROUP][:, j % GROUP, :]
 
-        def quantise(g):
-            x_words = x_tiles[g][:].bitcast(F32)
-            grouped = stage.tile([P, GROUP, P, PACK], BF16, align_bytes=64)
-            grouped_words = grouped[:].bitcast(F32)
-            for half in range(GROUP // 2):
-                xt = psum_x.tile([P, 2, 2, P], F32)
-                for a in range(2):
-                    for u in range(2):
-                        nc.tensor.transpose(
-                            xt[:, a, u, :], x_words[:, 2 * half + a, u:WORDS:2], ident
-                        )
-                nc.scalar.copy(
-                    out=grouped_words[:, 2 * half : 2 * half + 2, :, :],
-                    in_=xt[:].rearrange("p a u r -> p a r u"),
-                )
-            codes = stage.tile([P, GROUP * P], U32, align_bytes=64)
-            plane = stage.tile([P, GROUP * P], U8, align_bytes=64)
+        def quantise(duo):
+            x_words = x_tiles[duo * DUO // GROUP][:].bitcast(F32)
+            xt = psum_x.tile([P, DUO, 2, P], F32)
+            for a in range(DUO):
+                for u in range(2):
+                    nc.tensor.transpose(
+                        xt[:, a, u, :], x_words[:, (duo * DUO + a) % GROUP, u:WORDS:2], ident
+                    )
+            grouped = stage.tile([P, DUO, P, PACK], BF16, align_bytes=64)
+            nc.scalar.copy(
+                out=grouped[:].bitcast(F32), in_=xt[:].rearrange("p a u r -> p a r u")
+            )
+            codes = stage.tile([P, DUO * P], U32, align_bytes=64)
+            plane = stage.tile([P, DUO * P], U8, align_bytes=64)
             nc.vector.quantize_mx(
                 out=codes[:].bitcast(FP8X4),
                 scales=plane[:],
                 in_=grouped[:].rearrange("p a r t -> p (a r t)"),
             )
-            return codes, plane
+            quantised[duo] = (codes, plane)
 
-        def multiply(g, codes, plane):
-            row_sum = stats.tile([P, GROUP], F32)
-            row_sq = stats.tile([P, GROUP], F32)
-            for a in range(GROUP):
+        def multiply_and_add_bias(duo):
+            g = duo * DUO // GROUP
+            if duo * DUO % GROUP == 0:
+                row_sum[g] = stats.tile([P, GROUP], F32, name="row_sum")
+                row_sq[g] = stats.tile([P, GROUP], F32, name="row_sq")
+            codes, plane = quantised[duo]
+            banks = []
+            for a in range(DUO):
                 acc = psum_mx.tile([P, D], F32)
                 nc.tensor.matmul_mx(
                     out=acc[:],
@@ -110,29 +121,32 @@ def tile_dispatcher_pa_kernel(tc, inv, Wk_words, Wk_scales, bk, out):
                     start=True,
                     stop=True,
                 )
+                banks.append(acc)
+            for a in range(DUO):
+                j = duo * DUO + a
                 nc.vector.scalar_tensor_tensor(
-                    out=rows[g][:, a, :],
-                    in0=acc[:],
+                    out=row_tile(j),
+                    in0=banks[a][:],
                     scalar=1.0,
                     in1=bias[:],
                     op0=ALU.mult,
                     op1=ALU.add,
-                    accum_out=row_sum[:, a : a + 1],
+                    accum_out=row_sum[g][:, j % GROUP : j % GROUP + 1],
                 )
+
+        def square(duo):
+            for a in range(DUO):
+                j = duo * DUO + a
                 squares = stage.tile([P, D], F32, tag="unread")
                 nc.scalar.activation(
                     out=squares[:],
-                    in_=rows[g][:, a, :],
+                    in_=row_tile(j),
                     func=ACT.Square,
-                    accum_out=row_sq[:, a : a + 1],
+                    accum_out=row_sq[j // GROUP][:, j % GROUP : j % GROUP + 1],
                 )
-            return row_sum, row_sq
 
-        def scale_rows(g, row_sum, row_sq):
-            floored = stats.tile([P, GROUP], F32)
-            nc.vector.tensor_scalar_max(out=floored[:], in0=row_sq[:], scalar1=EPS * EPS)
-            norm = stats.tile([P, GROUP], F32)
-            nc.scalar.activation(out=norm[:], in_=floored[:], func=ACT.Sqrt)
+        def floor_and_clip(g):
+            nc.vector.tensor_scalar_max(out=row_sq[g][:], in0=row_sq[g][:], scalar1=EPS * EPS)
             nc.vector.tensor_scalar(
                 out=rows[g][:],
                 in0=rows[g][:],
@@ -141,12 +155,17 @@ def tile_dispatcher_pa_kernel(tc, inv, Wk_words, Wk_scales, bk, out):
                 op0=ALU.min,
                 op1=ALU.max,
             )
-            inv_norm = stats.tile([P, GROUP], F32)
-            nc.vector.reciprocal(out=inv_norm[:], in_=norm[:])
+
+        def take_root(g):
+            norm[g] = stats.tile([P, GROUP], F32, name="norm")
+            nc.scalar.activation(out=norm[g][:], in_=row_sq[g][:], func=ACT.Sqrt)
+
+        def weigh(g):
             weight = stats.tile([P, GROUP], F32)
-            nc.vector.tensor_mul(out=weight[:], in0=row_sum[:], in1=inv_norm[:])
+            nc.vector.reciprocal(out=weight[:], in_=norm[g][:])
+            nc.vector.tensor_mul(out=weight[:], in0=weight[:], in1=row_sum[g][:])
             for a in range(GROUP):
-                sign = 1.0 if (g * GROUP + a) % 2 == 0 else -1.0
+                sign = 1.0 if a % 2 == 0 else -1.0
                 nc.vector.tensor_scalar(
                     out=rows[g][:, a, :],
                     in0=rows[g][:, a, :],
@@ -156,44 +175,58 @@ def tile_dispatcher_pa_kernel(tc, inv, Wk_words, Wk_scales, bk, out):
                     op1=ALU.mult,
                 )
 
-        def sum_differences(b):
-            for s in range(SLICES):
-                cols = slice(s * P, (s + 1) * P)
-                et = psum_e.tile([P, GROUP, P], F32)
-                for i in range(GROUP):
-                    j = b * GROUP + i
-                    nc.tensor.matmul(
-                        out=et[:, i, :],
-                        lhsT=row_tile(j)[:, cols],
-                        rhs=ident,
-                        is_transpose=True,
-                        start=True,
-                        stop=False,
-                    )
-                    nc.tensor.matmul(
-                        out=et[:, i, :],
-                        lhsT=row_tile((j + 1) % TILES)[:, cols],
-                        rhs=ident if j + 1 < TILES else ident_next,
-                        is_transpose=True,
-                        start=False,
-                        stop=True,
-                    )
-                used = GROUP * P if b + 1 < GROUPS else GROUP * P - 1
-                sizes = stage.tile([P, GROUP * P], F32, tag="unread")
-                nc.scalar.activation(
-                    out=sizes[:, 0:used],
-                    in_=et[:].rearrange("p i r -> p (i r)")[:, 0:used],
-                    func=ACT.Abs,
-                    accum_out=part[:, s, b : b + 1],
+        def sum_differences(b, s):
+            cols = slice(s * P, (s + 1) * P)
+            et = psum_e.tile([P, GROUP, P], F32)
+            for i in range(GROUP):
+                j = b * GROUP + i
+                nc.tensor.matmul(
+                    out=et[:, i, :],
+                    lhsT=row_tile(j)[:, cols],
+                    rhs=ident,
+                    is_transpose=True,
+                    start=True,
+                    stop=False,
                 )
+                nc.tensor.matmul(
+                    out=et[:, i, :],
+                    lhsT=row_tile((j + 1) % TILES)[:, cols],
+                    rhs=ident if j + 1 < TILES else ident_next,
+                    is_transpose=True,
+                    start=False,
+                    stop=True,
+                )
+            return et
 
-        for g in range(GROUPS):
-            codes, plane = quantise(g)
-            row_sum, row_sq = multiply(g, codes, plane)
-            scale_rows(g, row_sum, row_sq)
-            if g >= 1:
-                sum_differences(g - 1)
-        sum_differences(GROUPS - 1)
+        def add_sizes(b, s, et):
+            used = GROUP * P if b + 1 < GROUPS else GROUP * P - 1
+            sizes = stage.tile([P, GROUP * P], F32, tag="unread")
+            nc.scalar.activation(
+                out=sizes[:, 0:used],
+                in_=et[:].rearrange("p i r -> p (i r)")[:, 0:used],
+                func=ACT.Abs,
+                accum_out=part[:, s, b : b + 1],
+            )
+
+        for step in range(-AHEAD, DUOS + DIFF_LAG):
+            before = step // 2 - 1
+            if 0 <= step < DUOS:
+                multiply_and_add_bias(step)
+            if 0 <= before < GROUPS and step % 2 == 0:
+                floor_and_clip(before)
+            if 0 <= before < GROUPS and step % 2 == 1:
+                weigh(before)
+            if step + AHEAD < DUOS:
+                quantise(step + AHEAD)
+            late = step - DIFF_LAG
+            if 0 <= late:
+                banks = [sum_differences(late // 2, 2 * (late % 2) + h) for h in range(2)]
+                for h in range(2):
+                    add_sizes(late // 2, 2 * (late % 2) + h, banks[h])
+            if 0 <= step < DUOS:
+                square(step)
+            if 0 <= before < GROUPS and step % 2 == 0:
+                take_root(before)
 
         total = keep.tile([P, SLICES], F32)
         nc.vector.tensor_reduce(out=total[:], in_=part[:], axis=mybir.AxisListType.X, op=ALU.add)

@@ -175,28 +175,31 @@ def tile_dispatcher_pa_kernel(tc, inv, Wk_words, Wk_scales, bk, out):
                     op1=ALU.mult,
                 )
 
-        def sum_differences(b, s):
-            cols = slice(s * P, (s + 1) * P)
-            et = psum_e.tile([P, GROUP, P], F32)
+        def sum_differences(b, first_slice):
+            ets = [psum_e.tile([P, GROUP, P], F32, name="et") for h in range(2)]
             for i in range(GROUP):
                 j = b * GROUP + i
-                nc.tensor.matmul(
-                    out=et[:, i, :],
-                    lhsT=row_tile(j)[:, cols],
-                    rhs=ident,
-                    is_transpose=True,
-                    start=True,
-                    stop=False,
-                )
-                nc.tensor.matmul(
-                    out=et[:, i, :],
-                    lhsT=row_tile((j + 1) % TILES)[:, cols],
-                    rhs=ident if j + 1 < TILES else ident_next,
-                    is_transpose=True,
-                    start=False,
-                    stop=True,
-                )
-            return et
+                for h in range(2):
+                    cols = slice((first_slice + h) * P, (first_slice + h + 1) * P)
+                    nc.tensor.matmul(
+                        out=ets[h][:, i, :],
+                        lhsT=row_tile(j)[:, cols],
+                        rhs=ident,
+                        is_transpose=True,
+                        start=True,
+                        stop=False,
+                    )
+                for h in range(2):
+                    cols = slice((first_slice + h) * P, (first_slice + h + 1) * P)
+                    nc.tensor.matmul(
+                        out=ets[h][:, i, :],
+                        lhsT=row_tile((j + 1) % TILES)[:, cols],
+                        rhs=ident if j + 1 < TILES else ident_next,
+                        is_transpose=True,
+                        start=False,
+                        stop=True,
+                    )
+            return ets
 
         def add_sizes(b, s, et):
             used = GROUP * P if b + 1 < GROUPS else GROUP * P - 1
@@ -220,7 +223,7 @@ def tile_dispatcher_pa_kernel(tc, inv, Wk_words, Wk_scales, bk, out):
                 quantise(step + AHEAD)
             late = step - DIFF_LAG
             if 0 <= late:
-                banks = [sum_differences(late // 2, 2 * (late % 2) + h) for h in range(2)]
+                banks = sum_differences(late // 2, 2 * (late % 2))
                 for h in range(2):
                     add_sizes(late // 2, 2 * (late % 2) + h, banks[h])
             if 0 <= step < DUOS:

@@ -211,8 +211,12 @@ def tile_dispatcher_pa_kernel(tc, inv, Wk_words, Wk_scales, bk, out):
                 accum_out=part[:, s, b : b + 1],
             )
 
-        for step in range(-AHEAD, DUOS + DIFF_LAG):
+        waiting = []
+        for step in range(-AHEAD, DUOS + DIFF_LAG + 1):
             before = step // 2 - 1
+            for b, s, et in waiting:
+                add_sizes(b, s, et)
+            waiting = []
             if 0 <= step < DUOS:
                 multiply_and_add_bias(step)
             if 0 <= before < GROUPS and step % 2 == 0:
@@ -222,10 +226,9 @@ def tile_dispatcher_pa_kernel(tc, inv, Wk_words, Wk_scales, bk, out):
             if step + AHEAD < DUOS:
                 quantise(step + AHEAD)
             late = step - DIFF_LAG
-            if 0 <= late:
+            if 0 <= late < DUOS:
                 banks = sum_differences(late // 2, 2 * (late % 2))
-                for h in range(2):
-                    add_sizes(late // 2, 2 * (late % 2) + h, banks[h])
+                waiting = [(late // 2, 2 * (late % 2) + h, banks[h]) for h in range(2)]
             if 0 <= step < DUOS:
                 square(step)
             if 0 <= before < GROUPS and step % 2 == 0:

@@ -56,7 +56,11 @@ def tile_dispatcher_pa_kernel(tc, inv, Wk_words, Wk_scales, bk, out):
 
         one = const.tile([P, 1], F32)
         nc.vector.memset(one[:], 1.0)
-        nc.scalar.activation(out=one[:], in_=one[:], func=ACT.Sqrt)
+        nc.scalar.activation(out=one[:], in_=one[:], func=ACT.Abs_reciprocal_sqrt)
+        floor = const.tile([P, 1], F32)
+        nc.vector.memset(floor[:], EPS * EPS)
+        minus_floor = const.tile([P, 1], F32)
+        nc.vector.memset(minus_floor[:], -EPS * EPS)
 
         x_tiles = []
         for g in range(GROUPS):
@@ -145,8 +149,7 @@ def tile_dispatcher_pa_kernel(tc, inv, Wk_words, Wk_scales, bk, out):
                     accum_out=row_sq[j // GROUP][:, j % GROUP : j % GROUP + 1],
                 )
 
-        def floor_and_clip(g):
-            nc.vector.tensor_scalar_max(out=row_sq[g][:], in0=row_sq[g][:], scalar1=EPS * EPS)
+        def clip(g):
             nc.vector.tensor_scalar(
                 out=rows[g][:],
                 in0=rows[g][:],
@@ -156,21 +159,29 @@ def tile_dispatcher_pa_kernel(tc, inv, Wk_words, Wk_scales, bk, out):
                 op1=ALU.max,
             )
 
-        def take_root(g):
+        def above_floor(g):
+            nc.scalar.activation(
+                out=row_sq[g][:], in_=row_sq[g][:], func=ACT.Relu, bias=minus_floor[:]
+            )
+
+        def invert_norm(g):
             norm[g] = stats.tile([P, GROUP], F32, name="norm")
-            nc.scalar.activation(out=norm[g][:], in_=row_sq[g][:], func=ACT.Sqrt)
+            nc.scalar.activation(
+                out=norm[g][:], in_=row_sq[g][:], func=ACT.Abs_reciprocal_sqrt, bias=floor[:]
+            )
+
+        def alternate_sign(g):
+            nc.scalar.activation(
+                out=norm[g][:, 1:GROUP:2], in_=norm[g][:, 1:GROUP:2], func=ACT.Copy, scale=-1.0
+            )
 
         def weigh(g):
-            weight = stats.tile([P, GROUP], F32)
-            nc.vector.reciprocal(out=weight[:], in_=norm[g][:])
-            nc.vector.tensor_mul(out=weight[:], in0=weight[:], in1=row_sum[g][:])
             for a in range(GROUP):
-                sign = 1.0 if a % 2 == 0 else -1.0
                 nc.vector.tensor_scalar(
                     out=rows[g][:, a, :],
                     in0=rows[g][:, a, :],
-                    scalar1=weight[:, a : a + 1],
-                    scalar2=sign / EPS,
+                    scalar1=norm[g][:, a : a + 1],
+                    scalar2=row_sum[g][:, a : a + 1],
                     op0=ALU.mult,
                     op1=ALU.mult,
                 )
@@ -214,13 +225,18 @@ def tile_dispatcher_pa_kernel(tc, inv, Wk_words, Wk_scales, bk, out):
         waiting = []
         for step in range(-AHEAD, DUOS + DIFF_LAG + 1):
             before = step // 2 - 1
+            ready = 0 <= before < GROUPS and step % 2 == 0
+            if ready:
+                above_floor(before)
             for b, s, et in waiting:
                 add_sizes(b, s, et)
             waiting = []
+            if ready:
+                invert_norm(before)
             if 0 <= step < DUOS:
                 multiply_and_add_bias(step)
-            if 0 <= before < GROUPS and step % 2 == 0:
-                floor_and_clip(before)
+            if ready:
+                clip(before)
             if 0 <= before < GROUPS and step % 2 == 1:
                 weigh(before)
             if step + AHEAD < DUOS:
@@ -229,10 +245,10 @@ def tile_dispatcher_pa_kernel(tc, inv, Wk_words, Wk_scales, bk, out):
             if 0 <= late < DUOS:
                 banks = sum_differences(late // 2, 2 * (late % 2))
                 waiting = [(late // 2, 2 * (late % 2) + h, banks[h]) for h in range(2)]
+            if ready:
+                alternate_sign(before)
             if 0 <= step < DUOS:
                 square(step)
-            if 0 <= before < GROUPS and step % 2 == 0:
-                take_root(before)
 
         total = keep.tile([P, SLICES], F32)
         nc.vector.tensor_reduce(out=total[:], in_=part[:], axis=mybir.AxisListType.X, op=ALU.add)
@@ -240,6 +256,8 @@ def tile_dispatcher_pa_kernel(tc, inv, Wk_words, Wk_scales, bk, out):
         for s in range(SLICES):
             nc.tensor.transpose(spread[:, s, :], total[:, s : s + 1].to_broadcast([P, P]), ident)
         result = keep.tile([P, D], F32)
-        nc.vector.tensor_copy(out=result[:], in_=spread[:].rearrange("p s r -> p (s r)"))
+        nc.vector.tensor_scalar_mul(
+            out=result[:], in0=spread[:].rearrange("p s r -> p (s r)"), scalar1=1.0 / EPS
+        )
         for r in range(D // P):
             nc.sync.dma_start(out=out[r * P : (r + 1) * P, :], in_=result[:])

@@ -176,8 +176,9 @@ def tile_dispatcher_pa_kernel(tc, inv, Wk_words, Wk_scales, bk, out):
             )
 
         def weigh(g):
+            engine = nc.vector if g == GROUPS - 1 else nc.gpsimd
             for a in range(GROUP):
-                nc.vector.tensor_scalar(
+                engine.tensor_scalar(
                     out=rows[g][:, a, :],
                     in0=rows[g][:, a, :],
                     scalar1=norm[g][:, a : a + 1],

@@ -78,6 +78,7 @@ def tile_dispatcher_pa_kernel(tc, inv, Wk_words, Wk_scales, bk, out):
 
         rows = [keep.tile([P, GROUP, D], F32, name="rows%d" % g) for g in range(GROUPS)]
         part = keep.tile([P, SLICES, GROUPS], F32)
+        turned = {}
         quantised = {}
         row_sum = {}
         row_sq = {}
@@ -86,7 +87,7 @@ def tile_dispatcher_pa_kernel(tc, inv, Wk_words, Wk_scales, bk, out):
         def row_tile(j):
             return rows[j // GROUP][:, j % GROUP, :]
 
-        def quantise(duo):
+        def turn(duo):
             x_words = x_tiles[duo * DUO // GROUP][:].bitcast(F32)
             xt = psum_x.tile([P, DUO, 2, P], F32)
             for a in range(DUO):
@@ -95,9 +96,13 @@ def tile_dispatcher_pa_kernel(tc, inv, Wk_words, Wk_scales, bk, out):
                         xt[:, a, u, :], x_words[:, (duo * DUO + a) % GROUP, u:WORDS:2], ident
                     )
             grouped = stage.tile([P, DUO, P, PACK], BF16, align_bytes=64)
-            nc.scalar.copy(
+            nc.vector.tensor_copy(
                 out=grouped[:].bitcast(F32), in_=xt[:].rearrange("p a u r -> p a r u")
             )
+            turned[duo] = grouped
+
+        def quantise(duo):
+            grouped = turned[duo]
             codes = stage.tile([P, DUO * P], U32, align_bytes=64)
             plane = stage.tile([P, DUO * P], U8, align_bytes=64)
             nc.vector.quantize_mx(
@@ -236,12 +241,14 @@ def tile_dispatcher_pa_kernel(tc, inv, Wk_words, Wk_scales, bk, out):
                 invert_norm(before)
             if 0 <= step < DUOS:
                 multiply_and_add_bias(step)
+            if 0 <= step + AHEAD - 1 < DUOS:
+                quantise(step + AHEAD - 1)
             if ready:
                 clip(before)
             if 0 <= before < GROUPS and step % 2 == 1:
                 weigh(before)
             if step + AHEAD < DUOS:
-                quantise(step + AHEAD)
+                turn(step + AHEAD)
             late = step - DIFF_LAG
             if 0 <= late < DUOS:
                 banks = sum_differences(late // 2, 2 * (late % 2))

@@ -96,9 +96,14 @@ def tile_dispatcher_pa_kernel(tc, inv, Wk_words, Wk_scales, bk, out):
                         xt[:, a, u, :], x_words[:, (duo * DUO + a) % GROUP, u:WORDS:2], ident
                     )
             grouped = stage.tile([P, DUO, P, PACK], BF16, align_bytes=64)
-            nc.vector.tensor_copy(
-                out=grouped[:].bitcast(F32), in_=xt[:].rearrange("p a u r -> p a r u")
-            )
+            if duo % 2 == 0:
+                nc.scalar.copy(
+                    out=grouped[:].bitcast(F32), in_=xt[:].rearrange("p a u r -> p a r u")
+                )
+            else:
+                nc.vector.tensor_copy(
+                    out=grouped[:].bitcast(F32), in_=xt[:].rearrange("p a u r -> p a r u")
+                )
             turned[duo] = grouped
 
         def quantise(duo):

@@ -24,6 +24,7 @@ DUO = 2
 DUOS = TILES // DUO
 AHEAD = 2
 DIFF_LAG = 5
+WARM_UP = 5
 SLICES = D // P
 WORDS = D // 2
 EPS = 1e-8
@@ -61,6 +62,18 @@ def tile_dispatcher_pa_kernel(tc, inv, Wk_words, Wk_scales, bk, out):
         nc.vector.memset(floor[:], EPS * EPS)
         minus_floor = const.tile([P, 1], F32)
         nc.vector.memset(minus_floor[:], -EPS * EPS)
+
+        filler = const.tile([P, D], BF16)
+        nc.vector.memset(filler[:], 1.0)
+
+        def keep_clock_up():
+            unused = psum_mx.tile([P, D], F32, name="acc")
+            nc.tensor.matmul(
+                out=unused[:], lhsT=filler[:, 0:P], rhs=filler[:], start=True, stop=True
+            )
+
+        for warm_up in range(WARM_UP):
+            keep_clock_up()
 
         x_tiles = []
         for g in range(GROUPS):
@@ -197,7 +210,7 @@ def tile_dispatcher_pa_kernel(tc, inv, Wk_words, Wk_scales, bk, out):
                     op1=ALU.mult,
                 )
 
-        def sum_differences(b, first_slice):
+        def sum_differences(b, first_slice, draining):
             ets = [psum_e.tile([P, GROUP, P], F32, name="et") for h in range(2)]
             for i in range(GROUP):
                 j = b * GROUP + i
@@ -221,6 +234,8 @@ def tile_dispatcher_pa_kernel(tc, inv, Wk_words, Wk_scales, bk, out):
                         start=False,
                         stop=True,
                     )
+                if draining and i % 2 == 1:
+                    keep_clock_up()
             return ets
 
         def add_sizes(b, s, et):
@@ -256,7 +271,7 @@ def tile_dispatcher_pa_kernel(tc, inv, Wk_words, Wk_scales, bk, out):
                 turn(step + AHEAD)
             late = step - DIFF_LAG
             if 0 <= late < DUOS:
-                banks = sum_differences(late // 2, 2 * (late % 2))
+                banks = sum_differences(late // 2, 2 * (late % 2), step >= DUOS)
                 waiting = [(late // 2, 2 * (late % 2) + h, banks[h]) for h in range(2)]
             if ready:
                 alternate_sign(before)

@@ -24,6 +24,7 @@ DUO = 2
 DUOS = TILES // DUO
 AHEAD = 2
 DIFF_LAG = 5
+EDGE = 8
 WARM_UP = 5
 SLICES = D // P
 WORDS = D // 2
@@ -109,7 +110,7 @@ def tile_dispatcher_pa_kernel(tc, inv, Wk_words, Wk_scales, bk, out):
                         xt[:, a, u, :], x_words[:, (duo * DUO + a) % GROUP, u:WORDS:2], ident
                     )
             grouped = stage.tile([P, DUO, P, PACK], BF16, align_bytes=64)
-            if duo % 2 == 0:
+            if duo < EDGE or (duo % 2 == 0 and duo < DUOS - EDGE):
                 nc.scalar.copy(
                     out=grouped[:].bitcast(F32), in_=xt[:].rearrange("p a u r -> p a r u")
                 )
@@ -248,6 +249,27 @@ def tile_dispatcher_pa_kernel(tc, inv, Wk_words, Wk_scales, bk, out):
                 accum_out=part[:, s, b : b + 1],
             )
 
+        total = keep.tile([P, SLICES], F32)
+        result = keep.tile([P, D], F32)
+
+        def finish(first_slice):
+            both = slice(first_slice, first_slice + SLICES // 2)
+            cols = slice(first_slice * P, (first_slice + SLICES // 2) * P)
+            nc.vector.tensor_reduce(
+                out=total[:, both], in_=part[:, both, :], axis=mybir.AxisListType.X, op=ALU.add
+            )
+            spread = psum_e.tile([P, SLICES // 2, P], F32, name="et")
+            for h in range(SLICES // 2):
+                s = first_slice + h
+                nc.tensor.transpose(
+                    spread[:, h, :], total[:, s : s + 1].to_broadcast([P, P]), ident
+                )
+            nc.vector.tensor_scalar_mul(
+                out=result[:, cols], in0=spread[:].rearrange("p s r -> p (s r)"), scalar1=1.0 / EPS
+            )
+            for r in range(D // P):
+                nc.sync.dma_start(out=out[r * P : (r + 1) * P, cols], in_=result[:, cols])
+
         waiting = []
         for step in range(-AHEAD, DUOS + DIFF_LAG + 1):
             before = step // 2 - 1
@@ -273,19 +295,11 @@ def tile_dispatcher_pa_kernel(tc, inv, Wk_words, Wk_scales, bk, out):
             if 0 <= late < DUOS:
                 banks = sum_differences(late // 2, 2 * (late % 2), step >= DUOS)
                 waiting = [(late // 2, 2 * (late % 2) + h, banks[h]) for h in range(2)]
+            if late == DUOS - 1:
+                finish(0)
             if ready:
                 alternate_sign(before)
             if 0 <= step < DUOS:
                 square(step)
 
-        total = keep.tile([P, SLICES], F32)
-        nc.vector.tensor_reduce(out=total[:], in_=part[:], axis=mybir.AxisListType.X, op=ALU.add)
-        spread = psum_e.tile([P, SLICES, P], F32, tag="et")
-        for s in range(SLICES):
-            nc.tensor.transpose(spread[:, s, :], total[:, s : s + 1].to_broadcast([P, P]), ident)
-        result = keep.tile([P, D], F32)
-        nc.vector.tensor_scalar_mul(
-            out=result[:], in0=spread[:].rearrange("p s r -> p (s r)"), scalar1=1.0 / EPS
-        )
-        for r in range(D // P):
-            nc.sync.dma_start(out=out[r * P : (r + 1) * P, :], in_=result[:])
+        finish(SLICES // 2)

@@ -22,7 +22,7 @@ GROUP = 4
 GROUPS = TILES // GROUP
 DUO = 2
 DUOS = TILES // DUO
-AHEAD = 2
+AHEAD = 4
 DIFF_LAG = 5
 EDGE = 8
 WARM_UP = 5
@@ -41,7 +41,9 @@ def tile_dispatcher_pa_kernel(tc, inv, Wk_words, Wk_scales, bk, out):
     with tc.tile_pool(name="const", bufs=1) as const, tc.tile_pool(
         name="keep", bufs=1
     ) as keep, tc.tile_pool(name="stage", bufs=4) as stage, tc.tile_pool(
-        name="stats", bufs=3
+        name="ahead", bufs=8
+    ) as ahead, tc.tile_pool(
+        name="stats", bufs=6
     ) as stats, tc.psum_pool(name="psum_x", bufs=2) as psum_x, tc.psum_pool(
         name="psum_mx", bufs=2
     ) as psum_mx, tc.psum_pool(name="psum_e", bufs=4) as psum_e, tc.manual_schedule():
@@ -59,10 +61,9 @@ def tile_dispatcher_pa_kernel(tc, inv, Wk_words, Wk_scales, bk, out):
         one = const.tile([P, 1], F32)
         nc.vector.memset(one[:], 1.0)
         nc.scalar.activation(out=one[:], in_=one[:], func=ACT.Abs_reciprocal_sqrt)
-        floor = const.tile([P, 1], F32)
-        nc.vector.memset(floor[:], EPS * EPS)
-        minus_floor = const.tile([P, 1], F32)
-        nc.vector.memset(minus_floor[:], -EPS * EPS)
+        signs = const.tile([P, GROUP], F32)
+        nc.vector.memset(signs[:, 0:GROUP:2], 1.0)
+        nc.vector.memset(signs[:, 1:GROUP:2], -1.0)
 
         filler = const.tile([P, D], BF16)
         nc.vector.memset(filler[:], 1.0)
@@ -93,6 +94,7 @@ def tile_dispatcher_pa_kernel(tc, inv, Wk_words, Wk_scales, bk, out):
         rows = [keep.tile([P, GROUP, D], F32, name="rows%d" % g) for g in range(GROUPS)]
         part = keep.tile([P, SLICES, GROUPS], F32)
         turned = {}
+        turning = {}
         quantised = {}
         row_sum = {}
         row_sq = {}
@@ -109,8 +111,12 @@ def tile_dispatcher_pa_kernel(tc, inv, Wk_words, Wk_scales, bk, out):
                     nc.tensor.transpose(
                         xt[:, a, u, :], x_words[:, (duo * DUO + a) % GROUP, u:WORDS:2], ident
                     )
-            grouped = stage.tile([P, DUO, P, PACK], BF16, align_bytes=64)
-            if duo < EDGE or (duo % 2 == 0 and duo < DUOS - EDGE):
+            turning[duo] = xt
+
+        def empty(duo, engine):
+            xt = turning[duo]
+            grouped = ahead.tile([P, DUO, P, PACK], BF16, align_bytes=64)
+            if engine == 0:
                 nc.scalar.copy(
                     out=grouped[:].bitcast(F32), in_=xt[:].rearrange("p a u r -> p a r u")
                 )
@@ -183,20 +189,18 @@ def tile_dispatcher_pa_kernel(tc, inv, Wk_words, Wk_scales, bk, out):
                 op1=ALU.max,
             )
 
-        def above_floor(g):
-            nc.scalar.activation(
-                out=row_sq[g][:], in_=row_sq[g][:], func=ACT.Relu, bias=minus_floor[:]
-            )
-
         def invert_norm(g):
             norm[g] = stats.tile([P, GROUP], F32, name="norm")
-            nc.scalar.activation(
-                out=norm[g][:], in_=row_sq[g][:], func=ACT.Abs_reciprocal_sqrt, bias=floor[:]
-            )
+            nc.scalar.activation(out=norm[g][:], in_=row_sq[g][:], func=ACT.Abs_reciprocal_sqrt)
 
-        def alternate_sign(g):
-            nc.scalar.activation(
-                out=norm[g][:, 1:GROUP:2], in_=norm[g][:, 1:GROUP:2], func=ACT.Copy, scale=-1.0
+        def bound_and_sign(g):
+            nc.vector.scalar_tensor_tensor(
+                out=norm[g][:],
+                in0=norm[g][:],
+                scalar=1.0 / EPS,
+                in1=signs[:],
+                op0=ALU.min,
+                op1=ALU.mult,
             )
 
         def weigh(g):
@@ -271,34 +275,53 @@ def tile_dispatcher_pa_kernel(tc, inv, Wk_words, Wk_scales, bk, out):
                 nc.sync.dma_start(out=out[r * P : (r + 1) * P, cols], in_=result[:, cols])
 
         waiting = []
-        for step in range(-AHEAD, DUOS + DIFF_LAG + 1):
+        for duo in range(3):
+            turn(duo)
+            empty(duo, 0)
+            if duo < 2:
+                quantise(duo)
+        turned_count = [3]
+        held = []
+        for step in range(0, DUOS + DIFF_LAG + 1):
             before = step // 2 - 1
             ready = 0 <= before < GROUPS and step % 2 == 0
-            if ready:
-                above_floor(before)
-            for b, s, et in waiting:
+            for n, (b, s, et) in enumerate(waiting):
                 add_sizes(b, s, et)
-            waiting = []
-            if ready:
+                if ready and n == 0:
+                    invert_norm(before)
+            if ready and not waiting:
                 invert_norm(before)
+            waiting = []
             if 0 <= step < DUOS:
                 multiply_and_add_bias(step)
-            if 0 <= step + AHEAD - 1 < DUOS:
-                quantise(step + AHEAD - 1)
+            while turned_count[0] <= min(step + AHEAD, DUOS - 1):
+                duo = turned_count[0]
+                turn(duo)
+                by_vector = duo >= EDGE and (duo % 2 == 1 or duo % 4 == 0)
+                if not by_vector:
+                    empty(duo, 0)
+                else:
+                    held.append(duo)
+                turned_count[0] += 1
+            if step % 2 == 1:
+                for duo in held:
+                    empty(duo, 1)
+                held = []
+            if step % 2 == 0:
+                for duo in (step + 2, step + 3):
+                    if duo < DUOS:
+                        quantise(duo)
             if ready:
                 clip(before)
+                bound_and_sign(before)
             if 0 <= before < GROUPS and step % 2 == 1:
                 weigh(before)
-            if step + AHEAD < DUOS:
-                turn(step + AHEAD)
             late = step - DIFF_LAG
             if 0 <= late < DUOS:
                 banks = sum_differences(late // 2, 2 * (late % 2), step >= DUOS)
                 waiting = [(late // 2, 2 * (late % 2) + h, banks[h]) for h in range(2)]
             if late == DUOS - 1:
                 finish(0)
-            if ready:
-                alternate_sign(before)
             if 0 <= step < DUOS:
                 square(step)
 

@@ -22,9 +22,10 @@ GROUP = 4
 GROUPS = TILES // GROUP
 DUO = 2
 DUOS = TILES // DUO
-AHEAD = 4
+EARLY = 2
+LEAD = 4
 DIFF_LAG = 5
-EDGE = 8
+EDGE = 10
 WARM_UP = 5
 SLICES = D // P
 WORDS = D // 2
@@ -42,11 +43,11 @@ def tile_dispatcher_pa_kernel(tc, inv, Wk_words, Wk_scales, bk, out):
         name="keep", bufs=1
     ) as keep, tc.tile_pool(name="stage", bufs=4) as stage, tc.tile_pool(
         name="ahead", bufs=8
-    ) as ahead, tc.tile_pool(
-        name="stats", bufs=6
-    ) as stats, tc.psum_pool(name="psum_x", bufs=2) as psum_x, tc.psum_pool(
-        name="psum_mx", bufs=2
-    ) as psum_mx, tc.psum_pool(name="psum_e", bufs=4) as psum_e, tc.manual_schedule():
+    ) as ahead, tc.tile_pool(name="stats", bufs=6) as stats, tc.psum_pool(
+        name="psum_x", bufs=2
+    ) as psum_x, tc.psum_pool(name="psum_mx", bufs=2) as psum_mx, tc.psum_pool(
+        name="psum_e", bufs=4
+    ) as psum_e, tc.manual_schedule():
         ident2 = const.tile([P, 2 * P], F32)
         make_identity(nc, ident2[:, 0:P])
         make_identity(nc, ident2[:, P : 2 * P])
@@ -61,9 +62,6 @@ def tile_dispatcher_pa_kernel(tc, inv, Wk_words, Wk_scales, bk, out):
         one = const.tile([P, 1], F32)
         nc.vector.memset(one[:], 1.0)
         nc.scalar.activation(out=one[:], in_=one[:], func=ACT.Abs_reciprocal_sqrt)
-        signs = const.tile([P, GROUP], F32)
-        nc.vector.memset(signs[:, 0:GROUP:2], 1.0)
-        nc.vector.memset(signs[:, 1:GROUP:2], -1.0)
 
         filler = const.tile([P, D], BF16)
         nc.vector.memset(filler[:], 1.0)
@@ -77,28 +75,31 @@ def tile_dispatcher_pa_kernel(tc, inv, Wk_words, Wk_scales, bk, out):
         for warm_up in range(WARM_UP):
             keep_clock_up()
 
-        x_tiles = []
-        for g in range(GROUPS):
-            x_sb = keep.tile([P, GROUP, D], BF16, name="x%d" % g)
-            nc.sync.dma_start(out=x_sb[:], in_=tokens[:, g * GROUP : (g + 1) * GROUP, :])
-            x_tiles.append(x_sb)
-            if g == 0:
-                nc.sync.dma_start(out=w_words[:].bitcast(I32), in_=Wk_words[0].bitcast(I32))
-                for q in range(4):
-                    nc.sync.dma_start(
-                        out=w_plane[32 * q : 32 * q + 4, :].bitcast(I32),
-                        in_=Wk_scales[0, 4 * q : 4 * q + 4, :].bitcast(I32),
-                    )
-                nc.sync.dma_start(out=bias[:], in_=bk.partition_broadcast(P))
+        x_tiles = [keep.tile([P, GROUP, D], BF16, name="x%d" % g) for g in range(GROUPS)]
+        nc.sync.dma_start(out=x_tiles[0][:, 0:DUO, :], in_=tokens[:, 0:DUO, :])
+        nc.sync.dma_start(out=w_words[:].bitcast(I32), in_=Wk_words[0].bitcast(I32))
+        for q in range(4):
+            nc.sync.dma_start(
+                out=w_plane[32 * q : 32 * q + 4, :].bitcast(I32),
+                in_=Wk_scales[0, 4 * q : 4 * q + 4, :].bitcast(I32),
+            )
+        nc.sync.dma_start(out=x_tiles[0][:, DUO:GROUP, :], in_=tokens[:, DUO:GROUP, :])
+        nc.sync.dma_start(out=x_tiles[1][:], in_=tokens[:, GROUP : 2 * GROUP, :])
+        nc.sync.dma_start(out=bias[:], in_=bk.partition_broadcast(P))
+        for g in range(2, GROUPS):
+            nc.sync.dma_start(
+                out=x_tiles[g][:], in_=tokens[:, g * GROUP : (g + 1) * GROUP, :]
+            )
 
         rows = [keep.tile([P, GROUP, D], F32, name="rows%d" % g) for g in range(GROUPS)]
         part = keep.tile([P, SLICES, GROUPS], F32)
-        turned = {}
         turning = {}
+        turned = {}
         quantised = {}
         row_sum = {}
         row_sq = {}
-        norm = {}
+        weight = {}
+        sums = {}
 
         def row_tile(j):
             return rows[j // GROUP][:, j % GROUP, :]
@@ -113,15 +114,15 @@ def tile_dispatcher_pa_kernel(tc, inv, Wk_words, Wk_scales, bk, out):
                     )
             turning[duo] = xt
 
-        def empty(duo, engine):
+        def empty(duo, by_vector):
             xt = turning[duo]
             grouped = ahead.tile([P, DUO, P, PACK], BF16, align_bytes=64)
-            if engine == 0:
-                nc.scalar.copy(
+            if by_vector:
+                nc.vector.tensor_copy(
                     out=grouped[:].bitcast(F32), in_=xt[:].rearrange("p a u r -> p a r u")
                 )
             else:
-                nc.vector.tensor_copy(
+                nc.scalar.copy(
                     out=grouped[:].bitcast(F32), in_=xt[:].rearrange("p a u r -> p a r u")
                 )
             turned[duo] = grouped
@@ -172,48 +173,59 @@ def tile_dispatcher_pa_kernel(tc, inv, Wk_words, Wk_scales, bk, out):
             for a in range(DUO):
                 j = duo * DUO + a
                 squares = stage.tile([P, D], F32, tag="unread")
-                nc.scalar.activation(
+                if j >= 63:
+                    nc.vector.scalar_tensor_tensor(
+                        out=squares[:], in0=row_tile(j), scalar=1.0, in1=row_tile(j), op0=ALU.mult, op1=ALU.mult,
+                        accum_out=row_sq[j // GROUP][:, j % GROUP : j % GROUP + 1])
+                else:
+                    nc.scalar.activation(
                     out=squares[:],
                     in_=row_tile(j),
                     func=ACT.Square,
                     accum_out=row_sq[j // GROUP][:, j % GROUP : j % GROUP + 1],
-                )
+                    )
 
-        def clip(g):
+        def invert_norm(g):
+            weight[g] = stats.tile([P, GROUP], F32, name="weight")
+            nc.scalar.activation(
+                out=weight[g][:], in_=row_sq[g][:], func=ACT.Abs_reciprocal_sqrt
+            )
+
+        def finish_weight(g):
+            nc.vector.scalar_tensor_tensor(
+                out=weight[g][:],
+                in0=weight[g][:],
+                scalar=1.0 / EPS,
+                in1=row_sum[g][:],
+                op0=ALU.min,
+                op1=ALU.mult,
+            )
+
+        def clip(g, first, last):
             nc.vector.tensor_scalar(
-                out=rows[g][:],
-                in0=rows[g][:],
+                out=rows[g][:, first:last, :],
+                in0=rows[g][:, first:last, :],
                 scalar1=CLIP,
                 scalar2=-CLIP,
                 op0=ALU.min,
                 op1=ALU.max,
             )
 
-        def invert_norm(g):
-            norm[g] = stats.tile([P, GROUP], F32, name="norm")
-            nc.scalar.activation(out=norm[g][:], in_=row_sq[g][:], func=ACT.Abs_reciprocal_sqrt)
-
-        def bound_and_sign(g):
-            nc.vector.scalar_tensor_tensor(
-                out=norm[g][:],
-                in0=norm[g][:],
-                scalar=1.0 / EPS,
-                in1=signs[:],
-                op0=ALU.min,
+        def weigh(j, engine):
+            engine.tensor_scalar(
+                out=row_tile(j),
+                in0=row_tile(j),
+                scalar1=weight[j // GROUP][:, j % GROUP : j % GROUP + 1],
+                scalar2=-1.0 if j % 2 else 1.0,
+                op0=ALU.mult,
                 op1=ALU.mult,
             )
 
-        def weigh(g):
-            engine = nc.vector if g == GROUPS - 1 else nc.gpsimd
-            for a in range(GROUP):
-                engine.tensor_scalar(
-                    out=rows[g][:, a, :],
-                    in0=rows[g][:, a, :],
-                    scalar1=norm[g][:, a : a + 1],
-                    scalar2=row_sum[g][:, a : a + 1],
-                    op0=ALU.mult,
-                    op1=ALU.mult,
-                )
+        def add_neighbours(j):
+            sums[j] = keep.tile([P, D], F32, name="sum%d" % j)
+            nc.vector.tensor_tensor(
+                out=sums[j][:], in0=row_tile(j), in1=row_tile(j + 1), op=ALU.add
+            )
 
         def sum_differences(b, first_slice, draining):
             ets = [psum_e.tile([P, GROUP, P], F32, name="et") for h in range(2)]
@@ -223,106 +235,124 @@ def tile_dispatcher_pa_kernel(tc, inv, Wk_words, Wk_scales, bk, out):
                     cols = slice((first_slice + h) * P, (first_slice + h + 1) * P)
                     nc.tensor.matmul(
                         out=ets[h][:, i, :],
-                        lhsT=row_tile(j)[:, cols],
+                        lhsT=sums[j][:, cols] if j in sums else row_tile(j)[:, cols],
                         rhs=ident,
                         is_transpose=True,
                         start=True,
-                        stop=False,
+                        stop=j in sums,
                     )
-                for h in range(2):
-                    cols = slice((first_slice + h) * P, (first_slice + h + 1) * P)
-                    nc.tensor.matmul(
-                        out=ets[h][:, i, :],
-                        lhsT=row_tile((j + 1) % TILES)[:, cols],
-                        rhs=ident if j + 1 < TILES else ident_next,
-                        is_transpose=True,
-                        start=False,
-                        stop=True,
-                    )
+                if j not in sums:
+                    for h in range(2):
+                        cols = slice((first_slice + h) * P, (first_slice + h + 1) * P)
+                        nc.tensor.matmul(
+                            out=ets[h][:, i, :],
+                            lhsT=row_tile((j + 1) % TILES)[:, cols],
+                            rhs=ident if j + 1 < TILES else ident_next,
+                            is_transpose=True,
+                            start=False,
+                            stop=True,
+                        )
                 if draining and i % 2 == 1:
                     keep_clock_up()
             return ets
 
         def add_sizes(b, s, et):
-            used = GROUP * P if b + 1 < GROUPS else GROUP * P - 1
+            first, last = 0, GROUP * P - (1 if b == GROUPS - 1 else 0)
             sizes = stage.tile([P, GROUP * P], F32, tag="unread")
             nc.scalar.activation(
-                out=sizes[:, 0:used],
-                in_=et[:].rearrange("p i r -> p (i r)")[:, 0:used],
+                out=sizes[:, first:last],
+                in_=et[:].rearrange("p i r -> p (i r)")[:, first:last],
                 func=ACT.Abs,
                 accum_out=part[:, s, b : b + 1],
             )
 
         total = keep.tile([P, SLICES], F32)
         result = keep.tile([P, D], F32)
+        LAST = GROUPS - 1
+
+        def sum_up(first_slice):
+            both = slice(first_slice, first_slice + SLICES // 2)
+            nc.vector.tensor_reduce(
+                out=total[:, both],
+                in_=part[:, both, 0:LAST],
+                axis=mybir.AxisListType.X,
+                op=ALU.add,
+            )
 
         def finish(first_slice):
-            both = slice(first_slice, first_slice + SLICES // 2)
             cols = slice(first_slice * P, (first_slice + SLICES // 2) * P)
-            nc.vector.tensor_reduce(
-                out=total[:, both], in_=part[:, both, :], axis=mybir.AxisListType.X, op=ALU.add
-            )
             spread = psum_e.tile([P, SLICES // 2, P], F32, name="et")
             for h in range(SLICES // 2):
                 s = first_slice + h
-                nc.tensor.transpose(
-                    spread[:, h, :], total[:, s : s + 1].to_broadcast([P, P]), ident
-                )
+                for n, sums_ in enumerate((total[:, s : s + 1], part[:, s, LAST : LAST + 1])):
+                    nc.tensor.matmul(
+                        out=spread[:, h, :],
+                        lhsT=sums_.to_broadcast([P, P]),
+                        rhs=ident,
+                        is_transpose=True,
+                        start=n == 0,
+                        stop=n == 1,
+                    )
             nc.vector.tensor_scalar_mul(
                 out=result[:, cols], in0=spread[:].rearrange("p s r -> p (s r)"), scalar1=1.0 / EPS
             )
             for r in range(D // P):
                 nc.sync.dma_start(out=out[r * P : (r + 1) * P, cols], in_=result[:, cols])
 
-        waiting = []
-        for duo in range(3):
+        for duo in range(EARLY):
             turn(duo)
-            empty(duo, 0)
+            empty(duo, False)
             if duo < 2:
                 quantise(duo)
-        turned_count = [3]
+        to_turn = list(range(EARLY, DUOS))
         held = []
-        for step in range(0, DUOS + DIFF_LAG + 1):
-            before = step // 2 - 1
-            ready = 0 <= before < GROUPS and step % 2 == 0
+        waiting = []
+        for step in range(DUOS + DIFF_LAG + 1):
+            g = step // 2 - 1
+            ready = 0 <= g < GROUPS and step % 2 == 0
+            if ready and not waiting:
+                invert_norm(g)
             for n, (b, s, et) in enumerate(waiting):
                 add_sizes(b, s, et)
                 if ready and n == 0:
-                    invert_norm(before)
-            if ready and not waiting:
-                invert_norm(before)
+                    invert_norm(g)
             waiting = []
-            if 0 <= step < DUOS:
+            if step < DUOS:
                 multiply_and_add_bias(step)
-            while turned_count[0] <= min(step + AHEAD, DUOS - 1):
-                duo = turned_count[0]
+            while to_turn and to_turn[0] <= step + LEAD:
+                duo = to_turn[0]
+                to_turn = to_turn[1:]
                 turn(duo)
-                by_vector = duo >= EDGE and (duo % 2 == 1 or duo % 4 == 0)
-                if not by_vector:
-                    empty(duo, 0)
-                else:
+                if duo >= EDGE and (duo % 2 == 1 or duo % 4 == 0):
                     held.append(duo)
-                turned_count[0] += 1
+                else:
+                    empty(duo, False)
             if step % 2 == 1:
                 for duo in held:
-                    empty(duo, 1)
+                    empty(duo, True)
                 held = []
             if step % 2 == 0:
                 for duo in (step + 2, step + 3):
                     if duo < DUOS:
                         quantise(duo)
             if ready:
-                clip(before)
-                bound_and_sign(before)
-            if 0 <= before < GROUPS and step % 2 == 1:
-                weigh(before)
+                finish_weight(g)
+                for first in range(0, GROUP, 2):
+                    clip(g, first, first + 2)
+                for a in range(GROUP):
+                    weigh(g * GROUP + a, nc.vector if g >= GROUPS - 1 else nc.gpsimd)
+                if g == GROUPS - 1:
+                    for j in (60, 61, 62,):
+                        add_neighbours(j)
             late = step - DIFF_LAG
             if 0 <= late < DUOS:
                 banks = sum_differences(late // 2, 2 * (late % 2), step >= DUOS)
                 waiting = [(late // 2, 2 * (late % 2) + h, banks[h]) for h in range(2)]
             if late == DUOS - 1:
+                sum_up(0)
+                sum_up(SLICES // 2)
                 finish(0)
-            if 0 <= step < DUOS:
+            if step < DUOS:
                 square(step)
 
         finish(SLICES // 2)

@@ -22,7 +22,7 @@ GROUP = 4
 GROUPS = TILES // GROUP
 DUO = 2
 DUOS = TILES // DUO
-EARLY = 2
+EARLY = 3
 LEAD = 4
 DIFF_LAG = 5
 EDGE = 10
@@ -323,7 +323,7 @@ def tile_dispatcher_pa_kernel(tc, inv, Wk_words, Wk_scales, bk, out):
                 duo = to_turn[0]
                 to_turn = to_turn[1:]
                 turn(duo)
-                if duo >= EDGE and (duo % 2 == 1 or duo % 4 == 0):
+                if duo >= EDGE and duo % 2 == 1:
                     held.append(duo)
                 else:
                     empty(duo, False)
@@ -337,10 +337,10 @@ def tile_dispatcher_pa_kernel(tc, inv, Wk_words, Wk_scales, bk, out):
                         quantise(duo)
             if ready:
                 finish_weight(g)
-                for first in range(0, GROUP, 2):
-                    clip(g, first, first + 2)
+                for first in range(0, GROUP, 4):
+                    clip(g, first, first + 4)
                 for a in range(GROUP):
-                    weigh(g * GROUP + a, nc.vector if g >= GROUPS - 1 else nc.gpsimd)
+                    weigh(g * GROUP + a, nc.vector if g >= GROUPS - 1 or a == 0 else nc.gpsimd)
                 if g == GROUPS - 1:
                     for j in (60, 61, 62,):
                         add_neighbours(j)

@@ -323,7 +323,7 @@ def tile_dispatcher_pa_kernel(tc, inv, Wk_words, Wk_scales, bk, out):
                 duo = to_turn[0]
                 to_turn = to_turn[1:]
                 turn(duo)
-                if duo >= EDGE and duo % 2 == 1:
+                if duo >= EDGE and (duo % 2 == 1 or duo % 4 == 0):
                     held.append(duo)
                 else:
                     empty(duo, False)
@@ -331,14 +331,14 @@ def tile_dispatcher_pa_kernel(tc, inv, Wk_words, Wk_scales, bk, out):
                 for duo in held:
                     empty(duo, True)
                 held = []
-            if step % 2 == 0:
-                for duo in (step + 2, step + 3):
-                    if duo < DUOS:
-                        quantise(duo)
+            if step % 2 == 0 and step + 2 < DUOS:
+                quantise(step + 2)
             if ready:
+                clip(g, 0, GROUP)
                 finish_weight(g)
-                for first in range(0, GROUP, 4):
-                    clip(g, first, first + 4)
+            if step % 2 == 0 and step + 3 < DUOS:
+                quantise(step + 3)
+            if ready:
                 for a in range(GROUP):
                     weigh(g * GROUP + a, nc.vector if g >= GROUPS - 1 or a == 0 else nc.gpsimd)
                 if g == GROUPS - 1:

@@ -37,12 +37,13 @@ FLOPS = 2 * TOKENS * D * D
 
 def tile_dispatcher_pa_kernel(tc, inv, Wk_words, Wk_scales, bk, out):
     nc = tc.nc
+    out_rows = out.rearrange("(r p) d -> p r d", p=P)
     tokens = inv.flatten_outer_dims().rearrange("(p j) k -> p j k", j=TILES)
 
     with tc.tile_pool(name="const", bufs=1) as const, tc.tile_pool(
         name="keep", bufs=1
     ) as keep, tc.tile_pool(name="stage", bufs=4) as stage, tc.tile_pool(
-        name="ahead", bufs=8
+        name="ahead", bufs=10
     ) as ahead, tc.tile_pool(name="stats", bufs=6) as stats, tc.psum_pool(
         name="psum_x", bufs=2
     ) as psum_x, tc.psum_pool(name="psum_mx", bufs=2) as psum_mx, tc.psum_pool(
@@ -229,30 +230,47 @@ def tile_dispatcher_pa_kernel(tc, inv, Wk_words, Wk_scales, bk, out):
 
         def sum_differences(b, first_slice, draining):
             ets = [psum_e.tile([P, GROUP, P], F32, name="et") for h in range(2)]
-            for i in range(GROUP):
+            def open_region(h, i):
                 j = b * GROUP + i
-                for h in range(2):
-                    cols = slice((first_slice + h) * P, (first_slice + h + 1) * P)
+                cols = slice((first_slice + h) * P, (first_slice + h + 1) * P)
+                nc.tensor.matmul(
+                    out=ets[h][:, i, :],
+                    lhsT=sums[j][:, cols] if j in sums else row_tile(j)[:, cols],
+                    rhs=ident,
+                    is_transpose=True,
+                    start=True,
+                    stop=j in sums,
+                )
+
+            def close_region(h, i):
+                j = b * GROUP + i
+                cols = slice((first_slice + h) * P, (first_slice + h + 1) * P)
+                if j not in sums:
                     nc.tensor.matmul(
                         out=ets[h][:, i, :],
-                        lhsT=sums[j][:, cols] if j in sums else row_tile(j)[:, cols],
-                        rhs=ident,
+                        lhsT=row_tile((j + 1) % TILES)[:, cols],
+                        rhs=ident if j + 1 < TILES else ident_next,
                         is_transpose=True,
-                        start=True,
-                        stop=j in sums,
+                        start=False,
+                        stop=True,
                     )
-                if j not in sums:
-                    for h in range(2):
-                        cols = slice((first_slice + h) * P, (first_slice + h + 1) * P)
-                        nc.tensor.matmul(
-                            out=ets[h][:, i, :],
-                            lhsT=row_tile((j + 1) % TILES)[:, cols],
-                            rhs=ident if j + 1 < TILES else ident_next,
-                            is_transpose=True,
-                            start=False,
-                            stop=True,
-                        )
-                if draining and i % 2 == 1:
+
+            if b == GROUPS - 1 and first_slice > 0:
+                for i in range(GROUP):
+                    open_region(0, i)
+                open_region(1, 0)
+                close_region(0, GROUP - 1)
+                for i in range(1, GROUP):
+                    open_region(1, i)
+                keep_clock_up()
+                close_region(1, GROUP - 1)
+                return ets
+            for i in range(GROUP):
+                for h in range(2):
+                    open_region(h, i)
+                for h in range(2):
+                    close_region(h, i)
+                if draining and i == 1:
                     keep_clock_up()
             return ets
 
@@ -279,10 +297,10 @@ def tile_dispatcher_pa_kernel(tc, inv, Wk_words, Wk_scales, bk, out):
                 op=ALU.add,
             )
 
-        def finish(first_slice):
-            cols = slice(first_slice * P, (first_slice + SLICES // 2) * P)
-            spread = psum_e.tile([P, SLICES // 2, P], F32, name="et")
-            for h in range(SLICES // 2):
+        def finish(first_slice, slices):
+            cols = slice(first_slice * P, (first_slice + slices) * P)
+            spread = psum_e.tile([P, slices, P], F32, name="et")
+            for h in range(slices):
                 s = first_slice + h
                 for n, sums_ in enumerate((total[:, s : s + 1], part[:, s, LAST : LAST + 1])):
                     nc.tensor.matmul(
@@ -296,8 +314,10 @@ def tile_dispatcher_pa_kernel(tc, inv, Wk_words, Wk_scales, bk, out):
             nc.vector.tensor_scalar_mul(
                 out=result[:, cols], in0=spread[:].rearrange("p s r -> p (s r)"), scalar1=1.0 / EPS
             )
-            for r in range(D // P):
-                nc.sync.dma_start(out=out[r * P : (r + 1) * P, cols], in_=result[:, cols])
+            nc.sync.dma_start(
+                out=out_rows[:, :, cols],
+                in_=result[:, cols].unsqueeze(1).broadcast_to([P, D // P, cols.stop - cols.start]),
+            )
 
         for duo in range(EARLY):
             turn(duo)
@@ -316,10 +336,12 @@ def tile_dispatcher_pa_kernel(tc, inv, Wk_words, Wk_scales, bk, out):
                 add_sizes(b, s, et)
                 if ready and n == 0:
                     invert_norm(g)
+                if b == GROUPS - 1 and s >= SLICES // 2:
+                    finish(s, 1)
             waiting = []
             if step < DUOS:
                 multiply_and_add_bias(step)
-            while to_turn and to_turn[0] <= step + LEAD:
+            while to_turn and to_turn[0] <= step + min(LEAD + 1 * max(0, step - 2), 6):
                 duo = to_turn[0]
                 to_turn = to_turn[1:]
                 turn(duo)
@@ -351,8 +373,6 @@ def tile_dispatcher_pa_kernel(tc, inv, Wk_words, Wk_scales, bk, out):
             if late == DUOS - 1:
                 sum_up(0)
                 sum_up(SLICES // 2)
-                finish(0)
+                finish(0, 2)
             if step < DUOS:
                 square(step)
-
-        finish(SLICES // 2)

import math

import concourse.mybir as mybir
from concourse.masks import make_identity

F32 = mybir.dt.float32
BF16 = mybir.dt.bfloat16
I32 = mybir.dt.int32
U32 = mybir.dt.uint32
U8 = mybir.dt.uint8
FP8X4 = mybir.dt.float8_e4m3fn_x4
FP4X4 = mybir.dt.float4_e2m1fn_x4
ALU = mybir.AluOpType
ACT = mybir.ActivationFunctionType

P = 128
PACK = 4
D = 512
TOKENS = 8192
TILES = TOKENS // P
GROUP = 4
GROUPS = TILES // GROUP
DUO = 2
DUOS = TILES // DUO
EARLY = 3
LEAD = 4
DIFF_LAG = 5
EDGE = 10
WARM_UP = 5
SLICES = D // P
WORDS = D // 2
EPS = 1e-8
CLIP = EPS / math.sqrt(D)

FLOPS = 2 * TOKENS * D * D


def tile_dispatcher_pa_kernel(tc, inv, Wk_words, Wk_scales, bk, out):
    nc = tc.nc
    out_rows = out.rearrange("(r p) d -> p r d", p=P)
    tokens = inv.flatten_outer_dims().rearrange("(p j) k -> p j k", j=TILES)

    with tc.tile_pool(name="const", bufs=1) as const, tc.tile_pool(
        name="keep", bufs=1
    ) as keep, tc.tile_pool(name="stage", bufs=4) as stage, tc.tile_pool(
        name="ahead", bufs=10
    ) as ahead, tc.tile_pool(name="stats", bufs=6) as stats, tc.psum_pool(
        name="psum_x", bufs=2
    ) as psum_x, tc.psum_pool(name="psum_mx", bufs=2) as psum_mx, tc.psum_pool(
        name="psum_e", bufs=4
    ) as psum_e, tc.manual_schedule():
        ident2 = const.tile([P, 2 * P], F32)
        make_identity(nc, ident2[:, 0:P])
        make_identity(nc, ident2[:, P : 2 * P])
        ident = ident2[:, 0:P]
        ident_next = ident2[:, 1 : P + 1]

        w_words = const.tile([P, 2 * D], U8, align_bytes=64)
        w_plane = const.tile([P, D], U8, align_bytes=64)
        bias = const.tile([P, D], BF16)
        nc.vector.memset(w_plane[:].bitcast(I32), 0)

        one = const.tile([P, 1], F32)
        nc.vector.memset(one[:], 1.0)
        nc.scalar.activation(out=one[:], in_=one[:], func=ACT.Abs_reciprocal_sqrt)

        filler = const.tile([P, D], BF16)
        nc.vector.memset(filler[:], 1.0)

        def keep_clock_up():
            unused = psum_mx.tile([P, D], F32, name="acc")
            nc.tensor.matmul(
                out=unused[:], lhsT=filler[:, 0:P], rhs=filler[:], start=True, stop=True
            )

        for warm_up in range(WARM_UP):
            keep_clock_up()

        x_tiles = [keep.tile([P, GROUP, D], BF16, name="x%d" % g) for g in range(GROUPS)]
        nc.sync.dma_start(out=x_tiles[0][:, 0:DUO, :], in_=tokens[:, 0:DUO, :])
        nc.sync.dma_start(out=w_words[:].bitcast(I32), in_=Wk_words[0].bitcast(I32))
        for q in range(4):
            nc.sync.dma_start(
                out=w_plane[32 * q : 32 * q + 4, :].bitcast(I32),
                in_=Wk_scales[0, 4 * q : 4 * q + 4, :].bitcast(I32),
            )
        nc.sync.dma_start(out=x_tiles[0][:, DUO:GROUP, :], in_=tokens[:, DUO:GROUP, :])
        nc.sync.dma_start(out=x_tiles[1][:], in_=tokens[:, GROUP : 2 * GROUP, :])
        nc.sync.dma_start(out=bias[:], in_=bk.partition_broadcast(P))
        for g in range(2, GROUPS):
            nc.sync.dma_start(
                out=x_tiles[g][:], in_=tokens[:, g * GROUP : (g + 1) * GROUP, :]
            )

        rows = [keep.tile([P, GROUP, D], F32, name="rows%d" % g) for g in range(GROUPS)]
        part = keep.tile([P, SLICES, GROUPS], F32)
        turning = {}
        turned = {}
        quantised = {}
        row_sum = {}
        row_sq = {}
        weight = {}
        sums = {}

        def row_tile(j):
            return rows[j // GROUP][:, j % GROUP, :]

        def turn(duo):
            x_words = x_tiles[duo * DUO // GROUP][:].bitcast(F32)
            xt = psum_x.tile([P, DUO, 2, P], F32)
            for a in range(DUO):
                for u in range(2):
                    nc.tensor.transpose(
                        xt[:, a, u, :], x_words[:, (duo * DUO + a) % GROUP, u:WORDS:2], ident
                    )
            turning[duo] = xt

        def empty(duo, by_vector):
            xt = turning[duo]
            grouped = ahead.tile([P, DUO, P, PACK], BF16, align_bytes=64)
            if by_vector:
                nc.vector.tensor_copy(
                    out=grouped[:].bitcast(F32), in_=xt[:].rearrange("p a u r -> p a r u")
                )
            else:
                nc.scalar.copy(
                    out=grouped[:].bitcast(F32), in_=xt[:].rearrange("p a u r -> p a r u")
                )
            turned[duo] = grouped

        def quantise(duo):
            grouped = turned[duo]
            codes = stage.tile([P, DUO * P], U32, align_bytes=64)
            plane = stage.tile([P, DUO * P], U8, align_bytes=64)
            nc.vector.quantize_mx(
                out=codes[:].bitcast(FP8X4),
                scales=plane[:],
                in_=grouped[:].rearrange("p a r t -> p (a r t)"),
            )
            quantised[duo] = (codes, plane)

        def multiply_and_add_bias(duo):
            g = duo * DUO // GROUP
            if duo * DUO % GROUP == 0:
                row_sum[g] = stats.tile([P, GROUP], F32, name="row_sum")
                row_sq[g] = stats.tile([P, GROUP], F32, name="row_sq")
            codes, plane = quantised[duo]
            banks = []
            for a in range(DUO):
                acc = psum_mx.tile([P, D], F32)
                nc.tensor.matmul_mx(
                    out=acc[:],
                    lhsT=codes[:, a * P : (a + 1) * P].bitcast(FP8X4),
                    lhsT_scale=plane[:, a * P : (a + 1) * P],
                    rhs=w_words[:].bitcast(FP4X4),
                    rhs_scale=w_plane[:],
                    start=True,
                    stop=True,
                )
                banks.append(acc)
            for a in range(DUO):
                j = duo * DUO + a
                nc.vector.scalar_tensor_tensor(
                    out=row_tile(j),
                    in0=banks[a][:],
                    scalar=1.0,
                    in1=bias[:],
                    op0=ALU.mult,
                    op1=ALU.add,
                    accum_out=row_sum[g][:, j % GROUP : j % GROUP + 1],
                )

        def square(duo):
            for a in range(DUO):
                j = duo * DUO + a
                squares = stage.tile([P, D], F32, tag="unread")
                if j >= 63:
                    nc.vector.scalar_tensor_tensor(
                        out=squares[:], in0=row_tile(j), scalar=1.0, in1=row_tile(j), op0=ALU.mult, op1=ALU.mult,
                        accum_out=row_sq[j // GROUP][:, j % GROUP : j % GROUP + 1])
                else:
                    nc.scalar.activation(
                    out=squares[:],
                    in_=row_tile(j),
                    func=ACT.Square,
                    accum_out=row_sq[j // GROUP][:, j % GROUP : j % GROUP + 1],
                    )

        def invert_norm(g):
            weight[g] = stats.tile([P, GROUP], F32, name="weight")
            nc.scalar.activation(
                out=weight[g][:], in_=row_sq[g][:], func=ACT.Abs_reciprocal_sqrt
            )

        def finish_weight(g):
            nc.vector.scalar_tensor_tensor(
                out=weight[g][:],
                in0=weight[g][:],
                scalar=1.0 / EPS,
                in1=row_sum[g][:],
                op0=ALU.min,
                op1=ALU.mult,
            )

        def clip(g, first, last):
            nc.vector.tensor_scalar(
                out=rows[g][:, first:last, :],
                in0=rows[g][:, first:last, :],
                scalar1=CLIP,
                scalar2=-CLIP,
                op0=ALU.min,
                op1=ALU.max,
            )

        def weigh(j, engine):
            engine.tensor_scalar(
                out=row_tile(j),
                in0=row_tile(j),
                scalar1=weight[j // GROUP][:, j % GROUP : j % GROUP + 1],
                scalar2=-1.0 if j % 2 else 1.0,
                op0=ALU.mult,
                op1=ALU.mult,
            )

        def add_neighbours(j):
            sums[j] = keep.tile([P, D], F32, name="sum%d" % j)
            nc.vector.tensor_tensor(
                out=sums[j][:], in0=row_tile(j), in1=row_tile(j + 1), op=ALU.add
            )

        def sum_differences(b, first_slice, draining):
            ets = [psum_e.tile([P, GROUP, P], F32, name="et") for h in range(2)]
            def open_region(h, i):
                j = b * GROUP + i
                cols = slice((first_slice + h) * P, (first_slice + h + 1) * P)
                nc.tensor.matmul(
                    out=ets[h][:, i, :],
                    lhsT=sums[j][:, cols] if j in sums else row_tile(j)[:, cols],
                    rhs=ident,
                    is_transpose=True,
                    start=True,
                    stop=j in sums,
                )

            def close_region(h, i):
                j = b * GROUP + i
                cols = slice((first_slice + h) * P, (first_slice + h + 1) * P)
                if j not in sums:
                    nc.tensor.matmul(
                        out=ets[h][:, i, :],
                        lhsT=row_tile((j + 1) % TILES)[:, cols],
                        rhs=ident if j + 1 < TILES else ident_next,
                        is_transpose=True,
                        start=False,
                        stop=True,
                    )

            if b == GROUPS - 1 and first_slice > 0:
                for i in range(GROUP):
                    open_region(0, i)
                open_region(1, 0)
                close_region(0, GROUP - 1)
                for i in range(1, GROUP):
                    open_region(1, i)
                keep_clock_up()
                close_region(1, GROUP - 1)
                return ets
            for i in range(GROUP):
                for h in range(2):
                    open_region(h, i)
                for h in range(2):
                    close_region(h, i)
                if draining and i == 1:
                    keep_clock_up()
            return ets

        def add_sizes(b, s, et):
            first, last = 0, GROUP * P - (1 if b == GROUPS - 1 else 0)
            sizes = stage.tile([P, GROUP * P], F32, tag="unread")
            nc.scalar.activation(
                out=sizes[:, first:last],
                in_=et[:].rearrange("p i r -> p (i r)")[:, first:last],
                func=ACT.Abs,
                accum_out=part[:, s, b : b + 1],
            )

        total = keep.tile([P, SLICES], F32)
        result = keep.tile([P, D], F32)
        LAST = GROUPS - 1

        def sum_up(first_slice):
            both = slice(first_slice, first_slice + SLICES // 2)
            nc.vector.tensor_reduce(
                out=total[:, both],
                in_=part[:, both, 0:LAST],
                axis=mybir.AxisListType.X,
                op=ALU.add,
            )

        def finish(first_slice, slices):
            cols = slice(first_slice * P, (first_slice + slices) * P)
            spread = psum_e.tile([P, slices, P], F32, name="et")
            for h in range(slices):
                s = first_slice + h
                for n, sums_ in enumerate((total[:, s : s + 1], part[:, s, LAST : LAST + 1])):
                    nc.tensor.matmul(
                        out=spread[:, h, :],
                        lhsT=sums_.to_broadcast([P, P]),
                        rhs=ident,
                        is_transpose=True,
                        start=n == 0,
                        stop=n == 1,
                    )
            nc.vector.tensor_scalar_mul(
                out=result[:, cols], in0=spread[:].rearrange("p s r -> p (s r)"), scalar1=1.0 / EPS
            )
            nc.sync.dma_start(
                out=out_rows[:, :, cols],
                in_=result[:, cols].unsqueeze(1).broadcast_to([P, D // P, cols.stop - cols.start]),
            )

        for duo in range(EARLY):
            turn(duo)
            empty(duo, False)
            if duo < 2:
                quantise(duo)
        to_turn = list(range(EARLY, DUOS))
        held = []
        waiting = []
        for step in range(DUOS + DIFF_LAG + 1):
            g = step // 2 - 1
            ready = 0 <= g < GROUPS and step % 2 == 0
            if ready and not waiting:
                invert_norm(g)
            for n, (b, s, et) in enumerate(waiting):
                add_sizes(b, s, et)
                if ready and n == 0:
                    invert_norm(g)
                if b == GROUPS - 1 and s >= SLICES // 2:
                    finish(s, 1)
            waiting = []
            if step < DUOS:
                multiply_and_add_bias(step)
            while to_turn and to_turn[0] <= step + min(LEAD + 1 * max(0, step - 2), 6):
                duo = to_turn[0]
                to_turn = to_turn[1:]
                turn(duo)
                if duo >= EDGE and (duo % 2 == 1 or duo % 4 == 0):
                    held.append(duo)
                else:
                    empty(duo, False)
            if step % 2 == 1:
                for duo in held:
                    empty(duo, True)
                held = []
            if step % 2 == 0 and step + 2 < DUOS:
                quantise(step + 2)
            if ready:
                clip(g, 0, GROUP)
                finish_weight(g)
            if step % 2 == 0 and step + 3 < DUOS:
                quantise(step + 3)
            if ready:
                for a in range(GROUP):
                    weigh(g * GROUP + a, nc.vector if g >= GROUPS - 1 or a == 0 else nc.gpsimd)
                if g == GROUPS - 1:
                    for j in (60, 61, 62,):
                        add_neighbours(j)
            late = step - DIFF_LAG
            if 0 <= late < DUOS:
                banks = sum_differences(late // 2, 2 * (late % 2), step >= DUOS)
                waiting = [(late // 2, 2 * (late % 2) + h, banks[h]) for h in range(2)]
            if late == DUOS - 1:
                sum_up(0)
                sum_up(SLICES // 2)
                finish(0, 2)
            if step < DUOS:
                square(step)
